import numpy as np
import ml_dtypes


def mxq(x, axis, fmt="e4m3"):
    dtype, down = {"e4m3": (ml_dtypes.float8_e4m3fn, 7), "e5m2": (ml_dtypes.float8_e5m2, 14)}[fmt]
    v = np.moveaxis(np.asarray(x, np.float32).astype(ml_dtypes.bfloat16).astype(np.float64), axis, -1)
    blocks = v.reshape(v.shape[:-1] + (-1, 32))
    amax = np.abs(blocks).max(-1, keepdims=True)
    byte = np.maximum(np.where(amax > 0, np.frexp(amax)[1] - 1 + 127, 0) - down, 1)
    scale = np.exp2(byte - 127.0)
    codes = (blocks / scale).astype(np.float32).astype(dtype).astype(np.float64)
    return np.moveaxis((codes * scale).reshape(v.shape), -1, axis)


WIDE = False


def mx_kscale(k):
    if not WIDE:
        return np.ones(k)
    levels = np.array([10, -10, 5, -5, 0])
    a = np.random.permutation(np.resize(levels, k // 512 * 4)).reshape(k // 512, 4)
    idx = np.arange(k)
    return np.exp2(a[idx // 512, idx % 128 // 32])


BF16 = ml_dtypes.bfloat16


def bf(x):
    return np.asarray(x, np.float32).astype(BF16)


def f64(x):
    return np.asarray(x).astype(np.float64)


B, L, D, H = 1, 4096, 512, 2


def setup_inputs():
    s = mx_kscale(D)
    return {"x": bf(np.random.standard_normal((B, L, D)) * s),
            "w": bf(np.random.standard_normal((H, D, D)) / np.sqrt(D) / s[:, None] * s[None, :])}


def reference(x, w):
    wq = mxq(f64(w), 1, "e4m3")
    xq = mxq(f64(x), 2, "e4m3")
    xs = (xq[None] @ wq[:, None]).reshape(H * B, L, D)
    return mxq(xs, 2, "e4m3") @ wq

@@ -1,0 +1,231 @@
+from contextlib import ExitStack
+
+import concourse.mybir as mybir
+from concourse.masks import make_identity
+
+BF16 = mybir.dt.bfloat16
+F32 = mybir.dt.float32
+U32 = mybir.dt.uint32
+U8 = mybir.dt.uint8
+FP8X4 = mybir.dt.float8_e4m3fn_x4
+
+P = 128
+PACK = 4
+HALVES = 2
+L, D, H = 4096, 512, 2
+BLOCKS = 4
+CHUNK = P * BLOCKS
+CHUNKS = L // CHUNK
+STEPS = CHUNKS * H
+LAG = 2
+
+FLOPS = 2 * H * 2 * L * D * D
+
+
+def tile_multiheadattention_pa_t_kernel(tc, x, w, out):
+    nc = tc.nc
+    x_chunks = x[0].rearrange("(c p j) k -> c p (j k)", p=P, j=BLOCKS)
+    out_chunks = out.rearrange("h (c p j) n -> h c p (j n)", p=P, j=BLOCKS)
+
+    with ExitStack() as ctx:
+        keep = ctx.enter_context(tc.tile_pool(name="keep", bufs=1))
+        x_pool = ctx.enter_context(tc.tile_pool(name="x_rows", bufs=CHUNKS))
+        w_stage = ctx.enter_context(tc.tile_pool(name="w_stage", bufs=2))
+        x_stage = ctx.enter_context(tc.tile_pool(name="x_stage", bufs=2))
+        xs_stage = ctx.enter_context(tc.tile_pool(name="xs_stage", bufs=3))
+        out_stage = ctx.enter_context(tc.tile_pool(name="out_stage", bufs=4))
+        xt_banks = ctx.enter_context(tc.psum_pool(name="xt_banks", bufs=2))
+        xs_banks = ctx.enter_context(tc.psum_pool(name="xs_banks", bufs=3))
+        out_banks = ctx.enter_context(tc.psum_pool(name="out_banks", bufs=3))
+
+        def empty_bank(turn, dst, bank):
+            if turn % 2 == 0:
+                nc.vector.tensor_copy(out=dst, in_=bank)
+            else:
+                nc.scalar.copy(out=dst, in_=bank)
+
+        x_rows = []
+        w_rows = []
+
+        def load_x(c):
+            rows = x_pool.tile([P, BLOCKS * D], BF16, tag="x_rows")
+            nc.sync.dma_start(out=rows[:], in_=x_chunks[c])
+            x_rows.append(rows)
+
+        def load_w(h):
+            rows = keep.tile([P, PACK, D], BF16, tag="w_rows%d" % h)
+            nc.sync.dma_start(
+                out=rows[:].rearrange("p (u e) n -> p u (e n)", e=HALVES),
+                in_=w[h].rearrange("(u p e) n -> p u (e n)", u=HALVES, e=HALVES),
+            )
+            w_rows.append(rows)
+
+        load_x(0)
+        for h in range(H):
+            load_w(h)
+        for c in range(1, CHUNKS):
+            load_x(c)
+
+        identity = keep.tile([P, P], F32)
+        make_identity(nc, identity[:])
+
+        w_stat_codes = keep.tile([P, H, D], U32, align_bytes=64)
+        w_stat_scales = keep.tile([P, H, D], U8, align_bytes=64)
+        w_move_codes = keep.tile([P, H, D], U32, align_bytes=64)
+        w_move_scales = keep.tile([P, H, D], U8, align_bytes=64)
+        w_grouped = {}
+
+        def group_w_stationary(h):
+            grouped = w_stage.tile([P, D * PACK], BF16, tag="w_stat", align_bytes=64)
+            half = D // HALVES
+            for u in range(HALVES):
+                nc.vector.tensor_copy(
+                    out=grouped[:, u * half * PACK : (u + 1) * half * PACK].rearrange(
+                        "p (e m t) -> p e m t", e=HALVES, t=PACK
+                    ),
+                    in_=w_rows[h][:, :, u * half : (u + 1) * half].rearrange(
+                        "p t (m e) -> p e m t", e=HALVES
+                    ),
+                )
+            w_grouped["stationary", h] = grouped
+
+        def group_w_moving(h):
+            grouped = w_stage.tile([P, D * PACK], BF16, tag="w_move", align_bytes=64)
+            nc.scalar.copy(
+                out=grouped[:].rearrange("p (n t) -> p n t", t=PACK),
+                in_=w_rows[h][:].rearrange("p t n -> p n t"),
+            )
+            w_grouped["moving", h] = grouped
+
+        def quantise_w(form, h, codes, scales):
+            nc.vector.quantize_mx(
+                out=codes[:, h, :].bitcast(FP8X4),
+                scales=scales[:, h, :],
+                in_=w_grouped[form, h][:],
+            )
+
+        x_grouped = {}
+        x_codes = {}
+        x_scales = {}
+
+        def transpose_x(c):
+            words = x_rows[c][:].bitcast(F32)
+            grouped = x_stage.tile([P, CHUNK * PACK], BF16, tag="x_grouped", align_bytes=64)
+            grouped_words = grouped[:].bitcast(F32)
+            words_in_row = D // HALVES
+            pair = 2
+            for b in range(BLOCKS // pair):
+                xt = xt_banks.tile([P, HALVES, pair * P], F32, tag="xt")
+                for i in range(pair):
+                    j = b * pair + i
+                    for u in range(HALVES):
+                        first = j * words_in_row + u * P
+                        nc.tensor.transpose(
+                            xt[:, u, i * P : (i + 1) * P], words[:, first : first + P], identity[:]
+                        )
+                width = pair * P * HALVES
+                nc.scalar.copy(
+                    out=grouped_words[:, b * width : (b + 1) * width].rearrange(
+                        "p (r u) -> p r u", u=HALVES
+                    ),
+                    in_=xt[:].rearrange("p u r -> p r u"),
+                )
+            x_grouped[c] = grouped
+
+        def quantise_x(c):
+            codes = x_stage.tile([P, CHUNK], U32, tag="x_codes", align_bytes=64)
+            scales = x_stage.tile([P, CHUNK], U8, tag="x_scales", align_bytes=64)
+            nc.vector.quantize_mx(out=codes[:].bitcast(FP8X4), scales=scales[:], in_=x_grouped[c][:])
+            x_codes[c] = codes
+            x_scales[c] = scales
+
+        xs_grouped = {}
+        xs_codes = {}
+        xs_scales = {}
+
+        def first_product(s, j):
+            c, h = divmod(s, H)
+            if j == 0:
+                grouped = xs_stage.tile([P, CHUNK * PACK], BF16, tag="xs_grouped", align_bytes=64)
+                xs_grouped[s] = grouped
+            rows = slice(j * P, (j + 1) * P)
+            xs_t = xs_banks.tile([P, PACK, P], F32, tag="xs_t")
+            for t in range(PACK):
+                cols = slice(t * P, (t + 1) * P)
+                nc.tensor.matmul_mx(
+                    out=xs_t[:, t, :],
+                    lhsT=w_stat_codes[:, h, cols].bitcast(FP8X4),
+                    lhsT_scale=w_stat_scales[:, h, cols],
+                    rhs=x_codes[c][:, rows].bitcast(FP8X4),
+                    rhs_scale=x_scales[c][:, rows],
+                    start=True,
+                    stop=True,
+                )
+            empty_bank(
+                j,
+                xs_grouped[s][:, j * P * PACK : (j + 1) * P * PACK].rearrange(
+                    "p (r t) -> p r t", t=PACK
+                ),
+                xs_t[:].rearrange("p t r -> p r t"),
+            )
+
+        def quantise_xs(s):
+            codes = xs_stage.tile([P, CHUNK], U32, tag="xs_codes", align_bytes=64)
+            scales = xs_stage.tile([P, CHUNK], U8, tag="xs_scales", align_bytes=64)
+            nc.vector.quantize_mx(out=codes[:].bitcast(FP8X4), scales=scales[:], in_=xs_grouped[s][:])
+            xs_codes[s] = codes
+            xs_scales[s] = scales
+
+        out_rows = {}
+
+        def second_product(s, j):
+            h = s % H
+            if j == 0:
+                result = out_stage.tile([P, BLOCKS, D], F32, tag="out_rows")
+                out_rows[s] = result
+            rows = slice(j * P, (j + 1) * P)
+            acc = out_banks.tile([P, D], F32, tag="acc")
+            nc.tensor.matmul_mx(
+                out=acc[:],
+                lhsT=xs_codes[s][:, rows].bitcast(FP8X4),
+                lhsT_scale=xs_scales[s][:, rows],
+                rhs=w_move_codes[:, h, :].bitcast(FP8X4),
+                rhs_scale=w_move_scales[:, h, :],
+                start=True,
+                stop=True,
+            )
+            empty_bank(j + 1, out_rows[s][:, j, :], acc[:])
+
+        def store(s):
+            c, h = divmod(s, H)
+            nc.sync.dma_start(out=out_chunks[h, c], in_=out_rows[s][:].rearrange("p j n -> p (j n)"))
+
+        transpose_x(0)
+        group_w_stationary(0)
+        quantise_x(0)
+        quantise_w("stationary", 0, w_stat_codes, w_stat_scales)
+
+        for s in range(STEPS + LAG):
+            c, h = divmod(s, H)
+            next_chunk = h == 0 and c + 1 < CHUNKS
+            if s + 1 < H:
+                group_w_stationary(s + 1)
+            if s < H:
+                group_w_moving(s)
+            if next_chunk:
+                transpose_x(c + 1)
+            for j in range(BLOCKS):
+                if s < STEPS:
+                    first_product(s, j)
+                if j == 0 and s + 1 < H:
+                    quantise_w("stationary", s + 1, w_stat_codes, w_stat_scales)
+                if j == 0 and 1 <= s <= STEPS:
+                    quantise_xs(s - 1)
+                if j == 1 and 1 <= s <= H:
+                    quantise_w("moving", s - 1, w_move_codes, w_move_scales)
+                if j == 2 and next_chunk:
+                    quantise_x(c + 1)
+                if s >= LAG:
+                    second_product(s - LAG, j)
+            if s >= LAG:
+                store(s - LAG)

@@ -11,6 +11,7 @@ FP8X4 = mybir.dt.float8_e4m3fn_x4
 
 P = 128
 PACK = 4
+PSUM_BANKS = 8
 HALVES = 2
 L, D, H = 4096, 512, 2
 BLOCKS = 4
@@ -18,6 +19,9 @@ CHUNK = P * BLOCKS
 CHUNKS = L // CHUNK
 STEPS = CHUNKS * H
 LAG = 2
+STORE_BLOCKS = 2
+ROUND = 5
+VECTOR_TURNS = (0, 2)
 
 FLOPS = 2 * H * 2 * L * D * D
 
@@ -34,12 +38,14 @@ def tile_multiheadattention_pa_t_kernel(tc, x, w, out):
         x_stage = ctx.enter_context(tc.tile_pool(name="x_stage", bufs=2))
         xs_stage = ctx.enter_context(tc.tile_pool(name="xs_stage", bufs=3))
         out_stage = ctx.enter_context(tc.tile_pool(name="out_stage", bufs=4))
-        xt_banks = ctx.enter_context(tc.psum_pool(name="xt_banks", bufs=2))
-        xs_banks = ctx.enter_context(tc.psum_pool(name="xs_banks", bufs=3))
-        out_banks = ctx.enter_context(tc.psum_pool(name="out_banks", bufs=3))
+        banks = ctx.enter_context(tc.psum_pool(name="banks", bufs=PSUM_BANKS))
 
-        def empty_bank(turn, dst, bank):
-            if turn % 2 == 0:
+        emptied = []
+
+        def empty_bank(dst, bank):
+            turn = len(emptied) % ROUND
+            emptied.append(turn)
+            if turn in VECTOR_TURNS:
                 nc.vector.tensor_copy(out=dst, in_=bank)
             else:
                 nc.scalar.copy(out=dst, in_=bank)
@@ -92,8 +98,8 @@ def tile_multiheadattention_pa_t_kernel(tc, x, w, out):
         def group_w_moving(h):
             grouped = w_stage.tile([P, D * PACK], BF16, tag="w_move", align_bytes=64)
             nc.scalar.copy(
-                out=grouped[:].rearrange("p (n t) -> p n t", t=PACK),
-                in_=w_rows[h][:].rearrange("p t n -> p n t"),
+                out=grouped[:].rearrange("p (c i t) -> p c t i", i=4, t=PACK),
+                in_=w_rows[h][:].rearrange("p t (c i) -> p c t i", i=4),
             )
             w_grouped["moving", h] = grouped
 
@@ -115,7 +121,7 @@ def tile_multiheadattention_pa_t_kernel(tc, x, w, out):
             words_in_row = D // HALVES
             pair = 2
             for b in range(BLOCKS // pair):
-                xt = xt_banks.tile([P, HALVES, pair * P], F32, tag="xt")
+                xt = banks.tile([P, HALVES, pair * P], F32, tag="bank")
                 for i in range(pair):
                     j = b * pair + i
                     for u in range(HALVES):
@@ -124,11 +130,11 @@ def tile_multiheadattention_pa_t_kernel(tc, x, w, out):
                             xt[:, u, i * P : (i + 1) * P], words[:, first : first + P], identity[:]
                         )
                 width = pair * P * HALVES
-                nc.scalar.copy(
-                    out=grouped_words[:, b * width : (b + 1) * width].rearrange(
+                empty_bank(
+                    grouped_words[:, b * width : (b + 1) * width].rearrange(
                         "p (r u) -> p r u", u=HALVES
                     ),
-                    in_=xt[:].rearrange("p u r -> p r u"),
+                    xt[:].rearrange("p u r -> p r u"),
                 )
             x_grouped[c] = grouped
 
@@ -149,7 +155,7 @@ def tile_multiheadattention_pa_t_kernel(tc, x, w, out):
                 grouped = xs_stage.tile([P, CHUNK * PACK], BF16, tag="xs_grouped", align_bytes=64)
                 xs_grouped[s] = grouped
             rows = slice(j * P, (j + 1) * P)
-            xs_t = xs_banks.tile([P, PACK, P], F32, tag="xs_t")
+            xs_t = banks.tile([P, PACK, P], F32, tag="bank")
             for t in range(PACK):
                 cols = slice(t * P, (t + 1) * P)
                 nc.tensor.matmul_mx(
@@ -162,7 +168,6 @@ def tile_multiheadattention_pa_t_kernel(tc, x, w, out):
                     stop=True,
                 )
             empty_bank(
-                j,
                 xs_grouped[s][:, j * P * PACK : (j + 1) * P * PACK].rearrange(
                     "p (r t) -> p r t", t=PACK
                 ),
@@ -184,7 +189,7 @@ def tile_multiheadattention_pa_t_kernel(tc, x, w, out):
                 result = out_stage.tile([P, BLOCKS, D], F32, tag="out_rows")
                 out_rows[s] = result
             rows = slice(j * P, (j + 1) * P)
-            acc = out_banks.tile([P, D], F32, tag="acc")
+            acc = banks.tile([P, D], F32, tag="bank")
             nc.tensor.matmul_mx(
                 out=acc[:],
                 lhsT=xs_codes[s][:, rows].bitcast(FP8X4),
@@ -194,12 +199,16 @@ def tile_multiheadattention_pa_t_kernel(tc, x, w, out):
                 start=True,
                 stop=True,
             )
-            empty_bank(j + 1, out_rows[s][:, j, :], acc[:])
+            empty_bank(out_rows[s][:, j, :], acc[:])
+            if (j + 1) % STORE_BLOCKS == 0:
+                c = s // H
+                first = j + 1 - STORE_BLOCKS
+                nc.sync.dma_start(
+                    out=out_chunks[h, c][:, first * D : (j + 1) * D],
+                    in_=out_rows[s][:, first : j + 1, :].rearrange("p j n -> p (j n)"),
+                )
 
-        def store(s):
-            c, h = divmod(s, H)
-            nc.sync.dma_start(out=out_chunks[h, c], in_=out_rows[s][:].rearrange("p j n -> p (j n)"))
-
+        ctx.enter_context(tc.manual_schedule())
         transpose_x(0)
         group_w_stationary(0)
         quantise_x(0)
@@ -227,5 +236,3 @@ def tile_multiheadattention_pa_t_kernel(tc, x, w, out):
                     quantise_x(c + 1)
                 if s >= LAG:
                     second_product(s - LAG, j)
-            if s >= LAG:
-                store(s - LAG)

@@ -14,11 +14,11 @@ PACK = 4
 PSUM_BANKS = 8
 HALVES = 2
 L, D, H = 4096, 512, 2
-BLOCKS = 4
+BLOCKS = 2
 CHUNK = P * BLOCKS
 CHUNKS = L // CHUNK
 STEPS = CHUNKS * H
-LAG = 2
+LAG = 3
 STORE_BLOCKS = 2
 ROUND = 5
 VECTOR_TURNS = (0, 2)
@@ -36,8 +36,8 @@ def tile_multiheadattention_pa_t_kernel(tc, x, w, out):
         x_pool = ctx.enter_context(tc.tile_pool(name="x_rows", bufs=CHUNKS))
         w_stage = ctx.enter_context(tc.tile_pool(name="w_stage", bufs=2))
         x_stage = ctx.enter_context(tc.tile_pool(name="x_stage", bufs=2))
-        xs_stage = ctx.enter_context(tc.tile_pool(name="xs_stage", bufs=3))
-        out_stage = ctx.enter_context(tc.tile_pool(name="out_stage", bufs=4))
+        xs_stage = ctx.enter_context(tc.tile_pool(name="xs_stage", bufs=LAG + 1))
+        out_stage = ctx.enter_context(tc.tile_pool(name="out_stage", bufs=6))
         banks = ctx.enter_context(tc.psum_pool(name="banks", bufs=PSUM_BANKS))
 
         emptied = []
@@ -66,9 +66,9 @@ def tile_multiheadattention_pa_t_kernel(tc, x, w, out):
             )
             w_rows.append(rows)
 
+        load_w(0)
         load_x(0)
-        for h in range(H):
-            load_w(h)
+        load_w(1)
         for c in range(1, CHUNKS):
             load_x(c)
 
@@ -209,30 +209,28 @@ def tile_multiheadattention_pa_t_kernel(tc, x, w, out):
                 )
 
         ctx.enter_context(tc.manual_schedule())
-        transpose_x(0)
         group_w_stationary(0)
-        quantise_x(0)
+        group_w_moving(0)
+        transpose_x(0)
         quantise_w("stationary", 0, w_stat_codes, w_stat_scales)
+        quantise_x(0)
+        group_w_stationary(1)
+        group_w_moving(1)
+        quantise_w("stationary", 1, w_stat_codes, w_stat_scales)
 
         for s in range(STEPS + LAG):
             c, h = divmod(s, H)
             next_chunk = h == 0 and c + 1 < CHUNKS
-            if s + 1 < H:
-                group_w_stationary(s + 1)
-            if s < H:
-                group_w_moving(s)
             if next_chunk:
                 transpose_x(c + 1)
             for j in range(BLOCKS):
-                if s < STEPS:
-                    first_product(s, j)
-                if j == 0 and s + 1 < H:
-                    quantise_w("stationary", s + 1, w_stat_codes, w_stat_scales)
-                if j == 0 and 1 <= s <= STEPS:
-                    quantise_xs(s - 1)
-                if j == 1 and 1 <= s <= H:
-                    quantise_w("moving", s - 1, w_move_codes, w_move_scales)
-                if j == 2 and next_chunk:
-                    quantise_x(c + 1)
                 if s >= LAG:
                     second_product(s - LAG, j)
+                if s < STEPS:
+                    first_product(s, j)
+                if j == 0 and 1 <= s <= STEPS:
+                    quantise_xs(s - 1)
+                if j == 1 and s < H:
+                    quantise_w("moving", s, w_move_codes, w_move_scales)
+                if j == 1 and next_chunk:
+                    quantise_x(c + 1)

@@ -19,7 +19,6 @@ CHUNK = P * BLOCKS
 CHUNKS = L // CHUNK
 STEPS = CHUNKS * H
 LAG = 3
-STORE_BLOCKS = 2
 ROUND = 5
 VECTOR_TURNS = (0, 2)
 
@@ -34,7 +33,6 @@ def tile_multiheadattention_pa_t_kernel(tc, x, w, out):
     with ExitStack() as ctx:
         keep = ctx.enter_context(tc.tile_pool(name="keep", bufs=1))
         x_pool = ctx.enter_context(tc.tile_pool(name="x_rows", bufs=CHUNKS))
-        w_stage = ctx.enter_context(tc.tile_pool(name="w_stage", bufs=2))
         x_stage = ctx.enter_context(tc.tile_pool(name="x_stage", bufs=2))
         xs_stage = ctx.enter_context(tc.tile_pool(name="xs_stage", bufs=LAG + 1))
         out_stage = ctx.enter_context(tc.tile_pool(name="out_stage", bufs=6))
@@ -75,17 +73,15 @@ def tile_multiheadattention_pa_t_kernel(tc, x, w, out):
         identity = keep.tile([P, P], F32)
         make_identity(nc, identity[:])
 
-        w_stat_codes = keep.tile([P, H, D], U32, align_bytes=64)
-        w_stat_scales = keep.tile([P, H, D], U8, align_bytes=64)
-        w_move_codes = keep.tile([P, H, D], U32, align_bytes=64)
-        w_move_scales = keep.tile([P, H, D], U8, align_bytes=64)
-        w_grouped = {}
+        w_codes = keep.tile([P, H, D], U32, align_bytes=64)
+        w_scales = keep.tile([P, H, D], U8, align_bytes=64)
+        w_grouped = []
 
-        def group_w_stationary(h):
-            grouped = w_stage.tile([P, D * PACK], BF16, tag="w_stat", align_bytes=64)
+        def group_w(h, copy):
+            grouped = keep.tile([P, D * PACK], BF16, tag="w_grouped%d" % h, align_bytes=64)
             half = D // HALVES
             for u in range(HALVES):
-                nc.vector.tensor_copy(
+                copy(
                     out=grouped[:, u * half * PACK : (u + 1) * half * PACK].rearrange(
                         "p (e m t) -> p e m t", e=HALVES, t=PACK
                     ),
@@ -93,21 +89,11 @@ def tile_multiheadattention_pa_t_kernel(tc, x, w, out):
                         "p t (m e) -> p e m t", e=HALVES
                     ),
                 )
-            w_grouped["stationary", h] = grouped
+            w_grouped.append(grouped)
 
-        def group_w_moving(h):
-            grouped = w_stage.tile([P, D * PACK], BF16, tag="w_move", align_bytes=64)
-            nc.scalar.copy(
-                out=grouped[:].rearrange("p (c i t) -> p c t i", i=4, t=PACK),
-                in_=w_rows[h][:].rearrange("p t (c i) -> p c t i", i=4),
-            )
-            w_grouped["moving", h] = grouped
-
-        def quantise_w(form, h, codes, scales):
+        def quantise_w(h):
             nc.vector.quantize_mx(
-                out=codes[:, h, :].bitcast(FP8X4),
-                scales=scales[:, h, :],
-                in_=w_grouped[form, h][:],
+                out=w_codes[:, h, :].bitcast(FP8X4), scales=w_scales[:, h, :], in_=w_grouped[h][:]
             )
 
         x_grouped = {}
@@ -117,25 +103,17 @@ def tile_multiheadattention_pa_t_kernel(tc, x, w, out):
         def transpose_x(c):
             words = x_rows[c][:].bitcast(F32)
             grouped = x_stage.tile([P, CHUNK * PACK], BF16, tag="x_grouped", align_bytes=64)
-            grouped_words = grouped[:].bitcast(F32)
-            words_in_row = D // HALVES
-            pair = 2
-            for b in range(BLOCKS // pair):
-                xt = banks.tile([P, HALVES, pair * P], F32, tag="bank")
-                for i in range(pair):
-                    j = b * pair + i
-                    for u in range(HALVES):
-                        first = j * words_in_row + u * P
-                        nc.tensor.transpose(
-                            xt[:, u, i * P : (i + 1) * P], words[:, first : first + P], identity[:]
-                        )
-                width = pair * P * HALVES
-                empty_bank(
-                    grouped_words[:, b * width : (b + 1) * width].rearrange(
-                        "p (r u) -> p r u", u=HALVES
-                    ),
-                    xt[:].rearrange("p u r -> p r u"),
-                )
+            xt = banks.tile([P, HALVES, CHUNK], F32, tag="bank")
+            for j in range(BLOCKS):
+                for u in range(HALVES):
+                    first = (j * HALVES + u) * P
+                    nc.tensor.transpose(
+                        xt[:, u, j * P : (j + 1) * P], words[:, first : first + P], identity[:]
+                    )
+            empty_bank(
+                grouped[:].bitcast(F32).rearrange("p (r u) -> p r u", u=HALVES),
+                xt[:].rearrange("p u r -> p r u"),
+            )
             x_grouped[c] = grouped
 
         def quantise_x(c):
@@ -160,8 +138,8 @@ def tile_multiheadattention_pa_t_kernel(tc, x, w, out):
                 cols = slice(t * P, (t + 1) * P)
                 nc.tensor.matmul_mx(
                     out=xs_t[:, t, :],
-                    lhsT=w_stat_codes[:, h, cols].bitcast(FP8X4),
-                    lhsT_scale=w_stat_scales[:, h, cols],
+                    lhsT=w_codes[:, h, cols].bitcast(FP8X4),
+                    lhsT_scale=w_scales[:, h, cols],
                     rhs=x_codes[c][:, rows].bitcast(FP8X4),
                     rhs_scale=x_scales[c][:, rows],
                     start=True,
@@ -184,7 +162,7 @@ def tile_multiheadattention_pa_t_kernel(tc, x, w, out):
         out_rows = {}
 
         def second_product(s, j):
-            h = s % H
+            c, h = divmod(s, H)
             if j == 0:
                 result = out_stage.tile([P, BLOCKS, D], F32, tag="out_rows")
                 out_rows[s] = result
@@ -194,29 +172,27 @@ def tile_multiheadattention_pa_t_kernel(tc, x, w, out):
                 out=acc[:],
                 lhsT=xs_codes[s][:, rows].bitcast(FP8X4),
                 lhsT_scale=xs_scales[s][:, rows],
-                rhs=w_move_codes[:, h, :].bitcast(FP8X4),
-                rhs_scale=w_move_scales[:, h, :],
+                rhs=w_codes[:, h, :].bitcast(FP8X4),
+                rhs_scale=w_scales[:, h, :],
                 start=True,
                 stop=True,
             )
-            empty_bank(out_rows[s][:, j, :], acc[:])
-            if (j + 1) % STORE_BLOCKS == 0:
-                c = s // H
-                first = j + 1 - STORE_BLOCKS
+            empty_bank(
+                out_rows[s][:, j, :].rearrange("p (u m e) -> p u m e", u=HALVES, e=HALVES),
+                acc[:].rearrange("p (u e m) -> p u m e", u=HALVES, e=HALVES),
+            )
+            if j == BLOCKS - 1:
                 nc.sync.dma_start(
-                    out=out_chunks[h, c][:, first * D : (j + 1) * D],
-                    in_=out_rows[s][:, first : j + 1, :].rearrange("p j n -> p (j n)"),
+                    out=out_chunks[h, c], in_=out_rows[s][:].rearrange("p j n -> p (j n)")
                 )
 
         ctx.enter_context(tc.manual_schedule())
-        group_w_stationary(0)
-        group_w_moving(0)
+        group_w(0, nc.vector.tensor_copy)
         transpose_x(0)
-        quantise_w("stationary", 0, w_stat_codes, w_stat_scales)
+        group_w(1, nc.scalar.copy)
+        quantise_w(0)
         quantise_x(0)
-        group_w_stationary(1)
-        group_w_moving(1)
-        quantise_w("stationary", 1, w_stat_codes, w_stat_scales)
+        quantise_w(1)
 
         for s in range(STEPS + LAG):
             c, h = divmod(s, H)
@@ -230,7 +206,5 @@ def tile_multiheadattention_pa_t_kernel(tc, x, w, out):
                     first_product(s, j)
                 if j == 0 and 1 <= s <= STEPS:
                     quantise_xs(s - 1)
-                if j == 1 and s < H:
-                    quantise_w("moving", s, w_move_codes, w_move_scales)
                 if j == 1 and next_chunk:
                     quantise_x(c + 1)

from contextlib import ExitStack

import concourse.mybir as mybir
from concourse.masks import make_identity

BF16 = mybir.dt.bfloat16
F32 = mybir.dt.float32
U32 = mybir.dt.uint32
U8 = mybir.dt.uint8
FP8X4 = mybir.dt.float8_e4m3fn_x4

P = 128
PACK = 4
PSUM_BANKS = 8
HALVES = 2
L, D, H = 4096, 512, 2
BLOCKS = 2
CHUNK = P * BLOCKS
CHUNKS = L // CHUNK
STEPS = CHUNKS * H
LAG = 3
ROUND = 5
VECTOR_TURNS = (0, 2)

FLOPS = 2 * H * 2 * L * D * D


def tile_multiheadattention_pa_t_kernel(tc, x, w, out):
    nc = tc.nc
    x_chunks = x[0].rearrange("(c p j) k -> c p (j k)", p=P, j=BLOCKS)
    out_chunks = out.rearrange("h (c p j) n -> h c p (j n)", p=P, j=BLOCKS)

    with ExitStack() as ctx:
        keep = ctx.enter_context(tc.tile_pool(name="keep", bufs=1))
        x_pool = ctx.enter_context(tc.tile_pool(name="x_rows", bufs=CHUNKS))
        x_stage = ctx.enter_context(tc.tile_pool(name="x_stage", bufs=2))
        xs_stage = ctx.enter_context(tc.tile_pool(name="xs_stage", bufs=LAG + 1))
        out_stage = ctx.enter_context(tc.tile_pool(name="out_stage", bufs=6))
        banks = ctx.enter_context(tc.psum_pool(name="banks", bufs=PSUM_BANKS))

        emptied = []

        def empty_bank(dst, bank):
            turn = len(emptied) % ROUND
            emptied.append(turn)
            if turn in VECTOR_TURNS:
                nc.vector.tensor_copy(out=dst, in_=bank)
            else:
                nc.scalar.copy(out=dst, in_=bank)

        x_rows = []
        w_rows = []

        def load_x(c):
            rows = x_pool.tile([P, BLOCKS * D], BF16, tag="x_rows")
            nc.sync.dma_start(out=rows[:], in_=x_chunks[c])
            x_rows.append(rows)

        def load_w(h):
            rows = keep.tile([P, PACK, D], BF16, tag="w_rows%d" % h)
            nc.sync.dma_start(
                out=rows[:].rearrange("p (u e) n -> p u (e n)", e=HALVES),
                in_=w[h].rearrange("(u p e) n -> p u (e n)", u=HALVES, e=HALVES),
            )
            w_rows.append(rows)

        load_w(0)
        load_x(0)
        load_w(1)
        for c in range(1, CHUNKS):
            load_x(c)

        identity = keep.tile([P, P], F32)
        make_identity(nc, identity[:])

        w_codes = keep.tile([P, H, D], U32, align_bytes=64)
        w_scales = keep.tile([P, H, D], U8, align_bytes=64)
        w_grouped = []

        def group_w(h, copy):
            grouped = keep.tile([P, D * PACK], BF16, tag="w_grouped%d" % h, align_bytes=64)
            half = D // HALVES
            for u in range(HALVES):
                copy(
                    out=grouped[:, u * half * PACK : (u + 1) * half * PACK].rearrange(
                        "p (e m t) -> p e m t", e=HALVES, t=PACK
                    ),
                    in_=w_rows[h][:, :, u * half : (u + 1) * half].rearrange(
                        "p t (m e) -> p e m t", e=HALVES
                    ),
                )
            w_grouped.append(grouped)

        def quantise_w(h):
            nc.vector.quantize_mx(
                out=w_codes[:, h, :].bitcast(FP8X4), scales=w_scales[:, h, :], in_=w_grouped[h][:]
            )

        x_grouped = {}
        x_codes = {}
        x_scales = {}

        def transpose_x(c):
            words = x_rows[c][:].bitcast(F32)
            grouped = x_stage.tile([P, CHUNK * PACK], BF16, tag="x_grouped", align_bytes=64)
            xt = banks.tile([P, HALVES, CHUNK], F32, tag="bank")
            for j in range(BLOCKS):
                for u in range(HALVES):
                    first = (j * HALVES + u) * P
                    nc.tensor.transpose(
                        xt[:, u, j * P : (j + 1) * P], words[:, first : first + P], identity[:]
                    )
            empty_bank(
                grouped[:].bitcast(F32).rearrange("p (r u) -> p r u", u=HALVES),
                xt[:].rearrange("p u r -> p r u"),
            )
            x_grouped[c] = grouped

        def quantise_x(c):
            codes = x_stage.tile([P, CHUNK], U32, tag="x_codes", align_bytes=64)
            scales = x_stage.tile([P, CHUNK], U8, tag="x_scales", align_bytes=64)
            nc.vector.quantize_mx(out=codes[:].bitcast(FP8X4), scales=scales[:], in_=x_grouped[c][:])
            x_codes[c] = codes
            x_scales[c] = scales

        xs_grouped = {}
        xs_codes = {}
        xs_scales = {}

        def first_product(s, j):
            c, h = divmod(s, H)
            if j == 0:
                grouped = xs_stage.tile([P, CHUNK * PACK], BF16, tag="xs_grouped", align_bytes=64)
                xs_grouped[s] = grouped
            rows = slice(j * P, (j + 1) * P)
            xs_t = banks.tile([P, PACK, P], F32, tag="bank")
            for t in range(PACK):
                cols = slice(t * P, (t + 1) * P)
                nc.tensor.matmul_mx(
                    out=xs_t[:, t, :],
                    lhsT=w_codes[:, h, cols].bitcast(FP8X4),
                    lhsT_scale=w_scales[:, h, cols],
                    rhs=x_codes[c][:, rows].bitcast(FP8X4),
                    rhs_scale=x_scales[c][:, rows],
                    start=True,
                    stop=True,
                )
            empty_bank(
                xs_grouped[s][:, j * P * PACK : (j + 1) * P * PACK].rearrange(
                    "p (r t) -> p r t", t=PACK
                ),
                xs_t[:].rearrange("p t r -> p r t"),
            )

        def quantise_xs(s):
            codes = xs_stage.tile([P, CHUNK], U32, tag="xs_codes", align_bytes=64)
            scales = xs_stage.tile([P, CHUNK], U8, tag="xs_scales", align_bytes=64)
            nc.vector.quantize_mx(out=codes[:].bitcast(FP8X4), scales=scales[:], in_=xs_grouped[s][:])
            xs_codes[s] = codes
            xs_scales[s] = scales

        out_rows = {}

        def second_product(s, j):
            c, h = divmod(s, H)
            if j == 0:
                result = out_stage.tile([P, BLOCKS, D], F32, tag="out_rows")
                out_rows[s] = result
            rows = slice(j * P, (j + 1) * P)
            acc = banks.tile([P, D], F32, tag="bank")
            nc.tensor.matmul_mx(
                out=acc[:],
                lhsT=xs_codes[s][:, rows].bitcast(FP8X4),
                lhsT_scale=xs_scales[s][:, rows],
                rhs=w_codes[:, h, :].bitcast(FP8X4),
                rhs_scale=w_scales[:, h, :],
                start=True,
                stop=True,
            )
            empty_bank(
                out_rows[s][:, j, :].rearrange("p (u m e) -> p u m e", u=HALVES, e=HALVES),
                acc[:].rearrange("p (u e m) -> p u m e", u=HALVES, e=HALVES),
            )
            if j == BLOCKS - 1:
                nc.sync.dma_start(
                    out=out_chunks[h, c], in_=out_rows[s][:].rearrange("p j n -> p (j n)")
                )

        ctx.enter_context(tc.manual_schedule())
        group_w(0, nc.vector.tensor_copy)
        transpose_x(0)
        group_w(1, nc.scalar.copy)
        quantise_w(0)
        quantise_x(0)
        quantise_w(1)

        for s in range(STEPS + LAG):
            c, h = divmod(s, H)
            next_chunk = h == 0 and c + 1 < CHUNKS
            if next_chunk:
                transpose_x(c + 1)
            for j in range(BLOCKS):
                if s >= LAG:
                    second_product(s - LAG, j)
                if s < STEPS:
                    first_product(s, j)
                if j == 0 and 1 <= s <= STEPS:
                    quantise_xs(s - 1)
                if j == 1 and next_chunk:
                    quantise_x(c + 1)
